import numpy as np
import ml_dtypes


def mxq(x, axis, fmt="e4m3"):
    dtype, down = {"e4m3": (ml_dtypes.float8_e4m3fn, 7), "e5m2": (ml_dtypes.float8_e5m2, 14)}[fmt]
    v = np.moveaxis(np.asarray(x, np.float32).astype(ml_dtypes.bfloat16).astype(np.float64), axis, -1)
    blocks = v.reshape(v.shape[:-1] + (-1, 32))
    amax = np.abs(blocks).max(-1, keepdims=True)
    byte = np.maximum(np.where(amax > 0, np.frexp(amax)[1] - 1 + 127, 0) - down, 1)
    scale = np.exp2(byte - 127.0)
    codes = (blocks / scale).astype(np.float32).astype(dtype).astype(np.float64)
    return np.moveaxis((codes * scale).reshape(v.shape), -1, axis)


WIDE = False


def mx_kscale(k):
    if not WIDE:
        return np.ones(k)
    levels = np.array([10, -10, 5, -5, 0])
    a = np.random.permutation(np.resize(levels, k // 512 * 4)).reshape(k // 512, 4)
    idx = np.arange(k)
    return np.exp2(a[idx // 512, idx % 128 // 32])


BF16 = ml_dtypes.bfloat16


def bf(x):
    return np.asarray(x, np.float32).astype(BF16)


def f64(x):
    return np.asarray(x).astype(np.float64)


B, P, D, DFF = 8, 64, 512, 1024


def sigmoid(v):
    return 1.0 / (1.0 + np.exp(-v))


def setup_inputs():
    s = mx_kscale(D)
    inp = {
        'Zi': bf(np.random.standard_normal((B, P, D)) * s),
        'Ci': bf(np.random.standard_normal((B, P, DFF))),
        'Mi': bf(np.random.standard_normal((B, P, DFF))),
        'Hi': bf(np.random.standard_normal((B, P, DFF))),
        'Ni': bf(np.random.uniform(0.5, 1.5, (B, P, DFF))),
        'm': bf(np.random.uniform(0.0, 1.0, (B, P, 1))),
    }
    for n in ('WI', 'WF', 'WO', 'WZ'):
        inp[n + '_w'] = bf(np.random.standard_normal((DFF, DFF)) * 0.7 / np.sqrt(DFF))
        inp[n + '_b'] = bf(np.random.standard_normal(DFF) * 0.3)
    for n in ('RI', 'RF', 'RO', 'RZ'):
        inp[n + '_w'] = bf(np.random.standard_normal((D, DFF)) * 0.7 / np.sqrt(D) / s[:, None])
        inp[n + '_b'] = bf(np.random.standard_normal(DFF) * 0.3)
    return inp


def reference(Zi, Ci, Mi, Hi, Ni, m,
              WI_w, WI_b, WF_w, WF_b, WO_w, WO_b, WZ_w, WZ_b,
              RI_w, RI_b, RF_w, RF_b, RO_w, RO_b, RZ_w, RZ_b):
    Zi, Ci, Mi, Hi, Ni, m = f64(Zi), f64(Ci), f64(Mi), f64(Hi), f64(Ni), f64(m)
    Wh = np.concatenate([f64(WI_w), f64(WF_w), f64(WO_w), f64(WZ_w)], axis=1)
    Wz = np.concatenate([f64(RI_w), f64(RF_w), f64(RO_w), f64(RZ_w)], axis=1)
    bias = np.concatenate([f64(WI_b) + f64(RI_b), f64(WF_b) + f64(RF_b), f64(WO_b) + f64(RO_b), f64(WZ_b) + f64(RZ_b)])
    gates = (mxq(Hi, 2, 'e4m3') @ mxq(Wh, 0, 'e4m3')) + (mxq(Zi, 2, 'e4m3') @ mxq(Wz, 0, 'e4m3')) + bias
    I_tilde, F_tilde, O_tilde, Z_tilde = np.split(gates, 4, axis=-1)

    M_t = np.maximum(F_tilde + Mi, I_tilde)
    I_t = np.exp(I_tilde - M_t)
    F_t = np.exp(F_tilde + Mi - M_t)
    O_t = sigmoid(O_tilde)
    N_t = F_t * Ni + I_t
    Z_t = np.tanh(Z_tilde)
    C_t = (Ci * F_t + Z_t * I_t) * m + (1.0 - m) * Ci
    H_t = O_t * (C_t / N_t) * m + (1.0 - m) * Hi
    return (C_t, M_t, H_t, N_t)

@@ -1,0 +1,442 @@
+from contextlib import ExitStack
+
+from concourse import mybir
+from concourse.masks import make_identity
+
+F32 = mybir.dt.float32
+BF16 = mybir.dt.bfloat16
+U32 = mybir.dt.uint32
+U8 = mybir.dt.uint8
+FP8X4 = mybir.dt.float8_e4m3fn_x4
+ALU = mybir.AluOpType
+ACT = mybir.ActivationFunctionType
+
+P = 128
+PACK = 4
+K_PASS = P * PACK
+BANK = 512
+TOKENS = 512
+TILES = TOKENS // P
+DFF = 1024
+HALF = DFF // 2
+BLOCKS = HALF // P
+GATE_BLOCKS = DFF // P
+PASSES = 3
+PAIRS = ((0, 1), (2, 3))
+FLOPS = 2 * TOKENS * (PASSES * K_PASS) * (4 * DFF)
+
+I, F, O, Z = 0, 1, 2, 3
+W_COLS = 4 * GATE_BLOCKS
+M_COL = 2 * W_COLS
+FINITE = 3.3895313892515355e38
+
+
+def tile_customlstmcell_kernel(
+    tc,
+    Zi, Ci, Mi, Hi, Ni, m,
+    WI_w, WI_b, WF_w, WF_b, WO_w, WO_b, WZ_w, WZ_b,
+    RI_w, RI_b, RF_w, RF_b, RO_w, RO_b, RZ_w, RZ_b,
+    out_0, out_1, out_2, out_3,
+):
+    nc = tc.nc
+    w_of = {I: WI_w, F: WF_w, O: WO_w, Z: WZ_w}
+    r_of = {I: RI_w, F: RF_w, O: RO_w, Z: RZ_w}
+    biases = [WI_b, WF_b, WO_b, WZ_b, RI_b, RF_b, RO_b, RZ_b]
+    state_of = {"mi": Mi, "ni": Ni, "ci": Ci}
+
+    def rows(ap):
+        return ap.rearrange("b p k -> (b p) k")
+
+    def tiled(ap):
+        return rows(ap).rearrange("(i q) k -> q i k", q=P)
+
+    c_out, m_out, h_out, n_out = rows(out_0), rows(out_1), rows(out_2), rows(out_3)
+
+    with ExitStack() as ctx:
+        consts = ctx.enter_context(tc.tile_pool(name="consts", bufs=1))
+        keep = ctx.enter_context(tc.tile_pool(name="keep", bufs=1))
+        codes = ctx.enter_context(tc.tile_pool(name="codes", bufs=1))
+        gate_pool = ctx.enter_context(tc.tile_pool(name="gate_pool", bufs=2 * BLOCKS))
+        raw_pool = ctx.enter_context(tc.tile_pool(name="raw_pool", bufs=4))
+        state_pool = ctx.enter_context(tc.tile_pool(name="state_pool", bufs=1))
+        grouped_pool = ctx.enter_context(tc.tile_pool(name="grouped_pool", bufs=3))
+        planes = ctx.enter_context(tc.tile_pool(name="planes", bufs=1))
+        pair_pool = ctx.enter_context(tc.tile_pool(name="pair_pool", bufs=2))
+        mx_banks = ctx.enter_context(tc.psum_pool(name="mx_banks", bufs=BLOCKS))
+        token_banks = ctx.enter_context(tc.psum_pool(name="token_banks", bufs=TILES))
+        ctx.enter_context(tc.manual_schedule())
+
+        hi_sb = keep.tile([P, TILES, DFF], BF16, name="hi_sb")
+        x_codes = keep.tile([P, PASSES, TOKENS], U32, name="x_codes", align_bytes=64)
+        x_scales = keep.tile([P, PASSES, TOKENS], U8, name="x_scales", align_bytes=64)
+        ident = consts.tile([P, P], F32, name="ident")
+        ident_bf = consts.tile([P, P], BF16, name="ident_bf")
+        neg_ident_bf = consts.tile([P, P], BF16, name="neg_ident_bf")
+        neg_m_diag = consts.tile([P, TILES, P], BF16, name="neg_m_diag")
+        vec_rows = consts.tile([P, P], BF16, name="vec_rows")
+        vec_rows_f = consts.tile([P, P], F32, name="vec_rows_f")
+        vec_cols = consts.tile([P, P], F32, name="vec_cols")
+        bias = consts.tile([P, W_COLS], F32, name="bias")
+        neg_bias_f = consts.tile([P, GATE_BLOCKS], F32, name="neg_bias_f")
+        half_bias_o = consts.tile([P, GATE_BLOCKS], F32, name="half_bias_o")
+        one_minus_m = consts.tile([P, TILES], F32, name="one_minus_m")
+        half_m = consts.tile([P, TILES], F32, name="half_m")
+
+        plane_a = planes.tile([P, 2 * TILES, HALF], F32, name="plane_a")
+        plane_b = planes.tile([P, 2 * TILES, HALF], F32, name="plane_b")
+        plane_c = planes.tile([P, 2 * TILES, HALF], F32, name="plane_c")
+        plane_d = planes.tile([P, 2 * TILES, HALF], F32, name="plane_d")
+
+        raw, grouped, w_codes, w_scales, state = {}, {}, {}, {}, {}
+        groups, gate_t, by_token, diff, rest_h = {}, {}, {}, {}, {}
+
+        def slot(plane, h, i):
+            return plane[:, TILES * h + i, :]
+
+        def half_plane(plane, h):
+            return plane[:, TILES * h : TILES * h + TILES, :].rearrange("p a b -> p (a b)")
+
+        def m_of(i):
+            return vec_cols[:, M_COL + i : M_COL + i + 1]
+
+        def gate_bias(g):
+            return slice(GATE_BLOCKS * g, GATE_BLOCKS * g + GATE_BLOCKS)
+
+        def half_cols(h):
+            return slice(h * HALF, h * HALF + HALF)
+
+        def tile_rows(i):
+            return slice(i * P, i * P + P)
+
+        def keep_finite(ap):
+            nc.vector.tensor_scalar(out=ap, in0=ap, scalar1=FINITE, scalar2=-FINITE, op0=ALU.min, op1=ALU.max)
+
+        def load_small():
+            make_identity(nc, ident[:])
+            nc.vector.memset(vec_rows[:], 0.0)
+            for v, vec in enumerate(biases):
+                nc.scalar.dma_start(out=vec_rows[gate_bias(v), :], in_=vec.rearrange("(r c) -> r c", c=P))
+            nc.scalar.dma_start(out=vec_rows[M_COL : M_COL + TILES, :], in_=m.rearrange("(r x) p o -> r (x p o)", x=2))
+
+        def load_activations():
+            nc.sync.dma_start(out=hi_sb[:], in_=tiled(Hi))
+            raw["zi"] = raw_pool.tile([P, TILES, K_PASS], BF16, tag="raw", name="zi_sb")
+            nc.sync.dma_start(out=raw["zi"][:], in_=tiled(Zi))
+
+        def quantise_activations():
+            hi_words = hi_sb[:].rearrange("q i k -> q (i k)").bitcast(F32).rearrange("q (n w u) -> q n w u", w=P, u=2)
+            zi_words = raw["zi"][:].rearrange("q i k -> q (i k)").bitcast(F32).rearrange("q (n w u) -> q n w u", w=P, u=2)
+            x_grouped = {}
+            for c in range(PASSES):
+                x_grouped[c] = grouped_pool.tile([P, 2, 2 * P * PACK], BF16, tag="grouped", name="x_grouped", align_bytes=64)
+                for two in range(2):
+                    bank = token_banks.tile([P, BANK], F32, tag="bank", name="x_bank")
+                    for u in range(2):
+                        for which in range(2):
+                            i = 2 * two + which
+                            words = hi_words[:, 2 * i + c, :, u] if c < 2 else zi_words[:, i, :, u]
+                            nc.tensor.transpose(bank[:, (2 * u + which) * P : (2 * u + which) * P + P], words, ident[:])
+                    dst = x_grouped[c][:, two, :].bitcast(F32).rearrange("p (r u) -> p r u", u=2)
+                    src = bank[:].rearrange("p (u r) -> p r u", u=2)
+                    if two == 0:
+                        nc.vector.tensor_copy(out=dst, in_=src)
+                    else:
+                        nc.scalar.copy(out=dst, in_=src)
+                if c > 0:
+                    quantise_pass(x_grouped, c - 1)
+            quantise_pass(x_grouped, PASSES - 1)
+
+        def quantise_pass(x_grouped, c):
+            nc.vector.quantize_mx(
+                out=x_codes[:, c, :].bitcast(FP8X4),
+                scales=x_scales[:, c, :],
+                in_=x_grouped[c][:].rearrange("p a b -> p (a b)"),
+            )
+
+        def prepare_biases():
+            nc.vector.tensor_copy(out=vec_rows_f[:], in_=vec_rows[:])
+            bank = token_banks.tile([P, BANK], F32, tag="bank", name="vec_bank")
+            nc.tensor.transpose(bank[:, 0:P], vec_rows_f[:], ident[:])
+            nc.vector.tensor_copy(out=vec_cols[:], in_=bank[:, 0:P])
+            nc.vector.tensor_tensor(out=bias[:], in0=vec_cols[:, 0:W_COLS], in1=vec_cols[:, W_COLS:M_COL], op=ALU.add)
+            nc.vector.tensor_scalar(out=neg_ident_bf[:], in0=ident[:], scalar1=-1.0, scalar2=None, op0=ALU.mult)
+            nc.vector.tensor_scalar(out=neg_bias_f[:], in0=bias[:, gate_bias(F)], scalar1=-1.0, scalar2=None, op0=ALU.mult)
+
+        def prepare_blends():
+            m_all = vec_cols[:, M_COL : M_COL + TILES]
+            keep_finite(m_all)
+            nc.vector.tensor_scalar(out=one_minus_m[:], in0=m_all, scalar1=-1.0, scalar2=1.0, op0=ALU.mult, op1=ALU.add)
+            nc.vector.tensor_scalar(out=half_m[:], in0=m_all, scalar1=0.5, scalar2=None, op0=ALU.mult)
+            nc.vector.tensor_scalar(out=half_bias_o[:], in0=bias[:, gate_bias(O)], scalar1=0.5, scalar2=None, op0=ALU.mult)
+            nc.vector.tensor_copy(out=ident_bf[:], in_=ident[:])
+            for i in range(TILES):
+                nc.vector.tensor_scalar(
+                    out=neg_m_diag[:, i, :], in0=ident[:], scalar1=m_of(i), scalar2=-1.0, op0=ALU.mult, op1=ALU.mult)
+
+        def load_slab(g, c):
+            src = w_of[g][K_PASS * c : K_PASS * c + K_PASS, :] if c < 2 else r_of[g]
+            raw[(g, c)] = raw_pool.tile([P, PACK, DFF], BF16, tag="raw", name="raw")
+            nc.sync.dma_start(out=raw[(g, c)][:], in_=src.rearrange("(p j) w -> p j w", j=PACK))
+
+        def regroup(g, c, h, engine):
+            dst = grouped[(g, c)][:, half_cols(h), :].rearrange("p (n r) j -> p n j r", r=4)
+            src = raw[(g, c)][:, :, half_cols(h)].rearrange("p j (n r) -> p n j r", r=4)
+            if engine == "scalar":
+                nc.scalar.copy(out=dst, in_=src)
+            else:
+                nc.vector.tensor_copy(out=dst, in_=src)
+
+        def quantise(g, c):
+            w_codes[(g, c)] = codes.tile([P, DFF], U32, name="w_codes%d_%d" % (g, c), align_bytes=64)
+            w_scales[(g, c)] = codes.tile([P, DFF], U8, name="w_scales%d_%d" % (g, c), align_bytes=64)
+            nc.vector.quantize_mx(
+                out=w_codes[(g, c)][:].bitcast(FP8X4),
+                scales=w_scales[(g, c)][:],
+                in_=grouped[(g, c)][:].rearrange("p w j -> p (w j)"),
+            )
+
+        def load_state(name, h):
+            state[(name, h)] = state_pool.tile([P, TILES, HALF], BF16, tag=name, name=name)
+            nc.sync.dma_start(out=state[(name, h)][:], in_=tiled(state_of[name])[:, :, half_cols(h)])
+
+        def products(g, h):
+            groups[(g, h)] = []
+            for b in range(BLOCKS):
+                cols = slice((BLOCKS * h + b) * P, (BLOCKS * h + b) * P + P)
+                group = mx_banks.tile([P, TOKENS], F32, tag="group", name="group")
+                for c in range(PASSES):
+                    nc.tensor.matmul_mx(
+                        out=group[:],
+                        lhsT=w_codes[(g, c)][:, cols].bitcast(FP8X4),
+                        lhsT_scale=w_scales[(g, c)][:, cols],
+                        rhs=x_codes[:, c, :].bitcast(FP8X4),
+                        rhs_scale=x_scales[:, c, :],
+                        start=(c == 0),
+                        stop=(c == PASSES - 1),
+                    )
+                groups[(g, h)].append(group)
+
+        def leave_psum(g, h):
+            gate_t[(g, h)] = []
+            for b in range(BLOCKS):
+                col = BLOCKS * h + b
+                block = gate_pool.tile([P, TOKENS], F32, tag="gate_t", name="gate_t")
+                group = groups[(g, h)][b]
+                if g == O:
+                    func, scale, shift = ACT.Tanh, 0.5, half_bias_o[:, col : col + 1]
+                elif g == F:
+                    func, scale, shift = ACT.Identity, -1.0, neg_bias_f[:, col : col + 1]
+                else:
+                    func, scale = (ACT.Tanh if g == Z else ACT.Identity), 1.0
+                    shift = bias[:, GATE_BLOCKS * g + col : GATE_BLOCKS * g + col + 1]
+                nc.scalar.activation(out=block[:], in_=group[:], func=func, bias=shift, scale=scale)
+                gate_t[(g, h)].append(block)
+
+        def back(g, h, tiles):
+            for i in tiles:
+                bank = token_banks.tile([P, HALF], F32, tag="bank", name="bank")
+                for b in range(BLOCKS):
+                    nc.tensor.transpose(bank[:, b * P : b * P + P], gate_t[(g, h)][b][:, tile_rows(i)], ident[:])
+                by_token[(g, h, i)] = bank
+
+        def difference(h, tiles):
+            for i in tiles:
+                bank = token_banks.tile([P, HALF], F32, tag="bank", name="bank")
+                for b in range(BLOCKS):
+                    cols = slice(b * P, b * P + P)
+                    a_t = gate_t[(I, h)][b][:, tile_rows(i)]
+                    neg_f_t = gate_t[(F, h)][b][:, tile_rows(i)]
+                    nc.tensor.matmul(out=bank[:, cols], lhsT=a_t, rhs=ident[:], is_transpose=True, start=True, stop=False)
+                    nc.tensor.matmul(out=bank[:, cols], lhsT=neg_f_t, rhs=ident[:], is_transpose=True, start=False, stop=False)
+                    nc.tensor.matmul(
+                        out=bank[:, cols], lhsT=neg_ident_bf[:], rhs=state[("mi", h)][:, i, cols], start=False, stop=True)
+                diff[(h, i)] = bank
+
+        def rest_of_h(h):
+            for i in range(TILES):
+                bank = token_banks.tile([P, HALF], F32, tag="bank", name="bank")
+                nc.tensor.matmul(out=bank[:], lhsT=ident_bf[:], rhs=hi_sb[:, i, half_cols(h)], start=True, stop=False)
+                nc.tensor.matmul(out=bank[:], lhsT=neg_m_diag[:, i, :], rhs=hi_sb[:, i, half_cols(h)], start=False, stop=True)
+                rest_h[(h, i)] = bank
+
+        def gates_if(h, pair):
+            for i in pair:
+                nc.scalar.activation(out=slot(plane_b, h, i), in_=diff[(h, i)][:], func=ACT.Relu, scale=-1.0)
+                nc.scalar.activation(out=slot(plane_c, h, i), in_=diff[(h, i)][:], func=ACT.Exp, scale=-1.0)
+            for i in pair:
+                nc.scalar.activation(out=slot(plane_a, h, i), in_=slot(plane_b, h, i), func=ACT.Exp, scale=-1.0)
+
+        def cell_m(h, pair):
+            for i in pair:
+                nc.vector.tensor_tensor(out=slot(plane_d, h, i), in0=by_token[(I, h, i)][:], in1=slot(plane_b, h, i), op=ALU.add)
+                nc.sync.dma_start(out=m_out[tile_rows(i), half_cols(h)], in_=slot(plane_d, h, i))
+
+        def cell_n(h, pair):
+            f_ni, m_f = {}, {}
+            for i in pair:
+                f_ni[i] = pair_pool.tile([P, HALF], F32, tag="first", name="f_ni")
+                nc.vector.scalar_tensor_tensor(
+                    out=f_ni[i][:], in0=slot(plane_c, h, i), scalar=1.0, in1=state[("ni", h)][:, i, :], op0=ALU.min, op1=ALU.mult)
+            for i in pair:
+                m_f[i] = pair_pool.tile([P, HALF], F32, tag="second", name="m_f")
+                nc.vector.tensor_scalar(
+                    out=m_f[i][:], in0=slot(plane_c, h, i), scalar1=1.0, scalar2=m_of(i), op0=ALU.min, op1=ALU.mult)
+            for i in pair:
+                nc.vector.tensor_tensor(out=slot(plane_c, h, i), in0=slot(plane_a, h, i), in1=f_ni[i][:], op=ALU.add)
+                nc.sync.dma_start(out=n_out[tile_rows(i), half_cols(h)], in_=slot(plane_c, h, i))
+            for i in pair:
+                nc.vector.scalar_tensor_tensor(
+                    out=slot(plane_b, h, i),
+                    in0=m_f[i][:],
+                    scalar=one_minus_m[:, i : i + 1],
+                    in1=state[("ci", h)][:, i, :],
+                    op0=ALU.add,
+                    op1=ALU.mult,
+                )
+
+        def abs_n(h, pair):
+            for i in pair:
+                nc.scalar.activation(out=slot(plane_d, h, i), in_=slot(plane_c, h, i), func=ACT.Abs)
+
+        def ln_n(h):
+            nc.scalar.activation(out=half_plane(plane_d, h), in_=half_plane(plane_d, h), func=ACT.Ln)
+
+        def inverse_square(h):
+            nc.scalar.activation(out=half_plane(plane_d, h), in_=half_plane(plane_d, h), func=ACT.Exp, scale=-2.0)
+
+        def cell_c(h, pair):
+            i_z = {}
+            for i in pair:
+                i_z[i] = pair_pool.tile([P, HALF], F32, tag="first", name="i_z")
+                nc.vector.tensor_tensor(out=i_z[i][:], in0=slot(plane_a, h, i), in1=by_token[(Z, h, i)][:], op=ALU.mult)
+            for i in pair:
+                nc.vector.scalar_tensor_tensor(
+                    out=slot(plane_a, h, i), in0=i_z[i][:], scalar=m_of(i), in1=slot(plane_b, h, i), op0=ALU.mult, op1=ALU.add)
+                nc.sync.dma_start(out=c_out[tile_rows(i), half_cols(h)], in_=slot(plane_a, h, i))
+            for i in pair:
+                nc.vector.tensor_tensor(out=slot(plane_b, h, i), in0=slot(plane_a, h, i), in1=slot(plane_c, h, i), op=ALU.mult)
+
+        def cell_o(h):
+            for i in range(TILES):
+                nc.vector.scalar_tensor_tensor(
+                    out=slot(plane_b, h, i), in0=by_token[(O, h, i)][:], scalar=1.0, in1=slot(plane_b, h, i), op0=ALU.add, op1=ALU.mult)
+
+        def cell_h(h, pair):
+            quotient = {}
+            for i in pair:
+                quotient[i] = pair_pool.tile([P, HALF], F32, tag="second", name="quotient")
+                nc.vector.tensor_tensor(out=quotient[i][:], in0=slot(plane_b, h, i), in1=slot(plane_d, h, i), op=ALU.mult)
+            for i in pair:
+                nc.vector.scalar_tensor_tensor(
+                    out=slot(plane_c, h, i),
+                    in0=quotient[i][:],
+                    scalar=half_m[:, i : i + 1],
+                    in1=rest_h[(h, i)][:],
+                    op0=ALU.mult,
+                    op1=ALU.add,
+                )
+                nc.sync.dma_start(out=h_out[tile_rows(i), half_cols(h)], in_=slot(plane_c, h, i))
+
+        slabs = [(g, c) for g in (F, I, Z, O) for c in range(PASSES)]
+        loads = slabs[:7] + [("mi", 0), slabs[7], ("ni", 0), ("ci", 0)] + slabs[8:]
+        whole_on_vector = (O, 1)
+        step = [0]
+
+        def next_load():
+            while loads:
+                what, index = loads.pop(0)
+                if what in state_of:
+                    load_state(what, index)
+                else:
+                    load_slab(what, index)
+                    break
+
+        def second_half(n):
+            if n < len(slabs):
+                g, c = slabs[n]
+                grouped[(g, c)] = grouped_pool.tile([P, DFF, PACK], BF16, tag="grouped", name="grouped", align_bytes=64)
+                regroup(g, c, 1, "vector" if (g, c) == whole_on_vector else "scalar")
+
+        def next_slab():
+            n = step[0]
+            step[0] = n + 1
+            second_half(n + 1)
+            if n < len(slabs):
+                regroup(slabs[n][0], slabs[n][1], 0, "vector")
+                next_load()
+            if n > 0:
+                quantise(slabs[n - 1][0], slabs[n - 1][1])
+
+        load_small()
+        load_activations()
+        for fill in range(3):
+            next_load()
+        quantise_activations()
+        next_load()
+        second_half(0)
+        next_slab()
+        next_slab()
+        prepare_biases()
+        next_slab()
+        next_slab()
+        products(F, 0)
+        next_slab()
+        leave_psum(F, 0)
+        next_slab()
+        next_slab()
+        products(I, 0)
+        leave_psum(I, 0)
+        keep_finite(state[("mi", 0)][:].rearrange("p a b -> p (a b)"))
+        prepare_blends()
+        keep_finite(hi_sb[:].rearrange("p a b -> p (a b)"))
+
+        for h in range(2):
+            ahead = ((F, 1), (I, 1)) if h == 0 else ((Z, 0), (Z, 1))
+            difference(h, PAIRS[0])
+            back(I, h, PAIRS[0])
+            gates_if(h, PAIRS[0])
+            next_slab()
+            cell_m(h, PAIRS[0])
+            difference(h, PAIRS[1])
+            back(I, h, PAIRS[1])
+            gates_if(h, PAIRS[1])
+            if h == 0:
+                load_state("mi", 1)
+            next_slab()
+            for which in range(2):
+                products(ahead[which][0], ahead[which][1])
+                leave_psum(ahead[which][0], ahead[which][1])
+                cell_n(h, PAIRS[which])
+                abs_n(h, PAIRS[which])
+                if which == 0:
+                    next_slab()
+                    cell_m(h, PAIRS[1])
+                    if h == 0:
+                        keep_finite(state[("mi", 1)][:].rearrange("p a b -> p (a b)"))
+            if h == 0:
+                load_state("ni", 1)
+                load_state("ci", 1)
+
+        back(Z, 0, range(TILES))
+        products(O, 0)
+        cell_c(0, PAIRS[0])
+        leave_psum(O, 0)
+        cell_c(0, PAIRS[1])
+        back(Z, 1, range(TILES))
+        products(O, 1)
+        ln_n(0)
+        ln_n(1)
+        cell_c(1, PAIRS[0])
+        cell_c(1, PAIRS[1])
+        back(O, 0, range(TILES))
+        inverse_square(0)
+        leave_psum(O, 1)
+        inverse_square(1)
+
+        for h in range(2):
+            if h == 1:
+                back(O, 1, range(TILES))
+            cell_o(h)
+            rest_of_h(h)
+            cell_h(h, PAIRS[0])
+            cell_h(h, PAIRS[1])

@@ -179,8 +179,8 @@ def tile_customlstmcell_kernel(
             nc.sync.dma_start(out=raw[(g, c)][:], in_=src.rearrange("(p j) w -> p j w", j=PACK))
 
         def regroup(g, c, h, engine):
-            dst = grouped[(g, c)][:, half_cols(h), :].rearrange("p (n r) j -> p n j r", r=4)
-            src = raw[(g, c)][:, :, half_cols(h)].rearrange("p j (n r) -> p n j r", r=4)
+            dst = grouped[(g, c)][:, half_cols(h), :].rearrange("p (n r) j -> p n j r", r=8)
+            src = raw[(g, c)][:, :, half_cols(h)].rearrange("p j (n r) -> p n j r", r=8)
             if engine == "scalar":
                 nc.scalar.copy(out=dst, in_=src)
             else:
@@ -328,14 +328,14 @@ def tile_customlstmcell_kernel(
                 nc.vector.tensor_tensor(out=quotient[i][:], in0=slot(plane_b, h, i), in1=slot(plane_d, h, i), op=ALU.mult)
             for i in pair:
                 nc.vector.scalar_tensor_tensor(
-                    out=slot(plane_c, h, i),
+                    out=slot(plane_b, h, i),
                     in0=quotient[i][:],
                     scalar=half_m[:, i : i + 1],
                     in1=rest_h[(h, i)][:],
                     op0=ALU.mult,
                     op1=ALU.add,
                 )
-                nc.sync.dma_start(out=h_out[tile_rows(i), half_cols(h)], in_=slot(plane_c, h, i))
+                nc.sync.dma_start(out=h_out[tile_rows(i), half_cols(h)], in_=slot(plane_b, h, i))
 
         slabs = [(g, c) for g in (F, I, Z, O) for c in range(PASSES)]
         loads = slabs[:7] + [("mi", 0), slabs[7], ("ni", 0), ("ci", 0)] + slabs[8:]

@@ -70,9 +70,7 @@ def tile_customlstmcell_kernel(
         x_codes = keep.tile([P, PASSES, TOKENS], U32, name="x_codes", align_bytes=64)
         x_scales = keep.tile([P, PASSES, TOKENS], U8, name="x_scales", align_bytes=64)
         ident = consts.tile([P, P], F32, name="ident")
-        ident_bf = consts.tile([P, P], BF16, name="ident_bf")
         neg_ident_bf = consts.tile([P, P], BF16, name="neg_ident_bf")
-        neg_m_diag = consts.tile([P, TILES, P], BF16, name="neg_m_diag")
         vec_rows = consts.tile([P, P], BF16, name="vec_rows")
         vec_rows_f = consts.tile([P, P], F32, name="vec_rows_f")
         vec_cols = consts.tile([P, P], F32, name="vec_cols")
@@ -164,14 +162,9 @@ def tile_customlstmcell_kernel(
 
         def prepare_blends():
             m_all = vec_cols[:, M_COL : M_COL + TILES]
-            keep_finite(m_all)
             nc.vector.tensor_scalar(out=one_minus_m[:], in0=m_all, scalar1=-1.0, scalar2=1.0, op0=ALU.mult, op1=ALU.add)
             nc.vector.tensor_scalar(out=half_m[:], in0=m_all, scalar1=0.5, scalar2=None, op0=ALU.mult)
             nc.vector.tensor_scalar(out=half_bias_o[:], in0=bias[:, gate_bias(O)], scalar1=0.5, scalar2=None, op0=ALU.mult)
-            nc.vector.tensor_copy(out=ident_bf[:], in_=ident[:])
-            for i in range(TILES):
-                nc.vector.tensor_scalar(
-                    out=neg_m_diag[:, i, :], in0=ident[:], scalar1=m_of(i), scalar2=-1.0, op0=ALU.mult, op1=ALU.mult)
 
         def load_slab(g, c):
             src = w_of[g][K_PASS * c : K_PASS * c + K_PASS, :] if c < 2 else r_of[g]
@@ -199,14 +192,17 @@ def tile_customlstmcell_kernel(
             state[(name, h)] = state_pool.tile([P, TILES, HALF], BF16, tag=name, name=name)
             nc.sync.dma_start(out=state[(name, h)][:], in_=tiled(state_of[name])[:, :, half_cols(h)])
 
-        def products(g, h):
-            groups[(g, h)] = []
+        def products(g, h, passes=range(PASSES)):
+            if (g, h) not in groups:
+                groups[(g, h)] = []
+                for b in range(BLOCKS):
+                    group = mx_banks.tile([P, TOKENS], F32, tag="group", name="group")
+                    groups[(g, h)].append(group)
             for b in range(BLOCKS):
                 cols = slice((BLOCKS * h + b) * P, (BLOCKS * h + b) * P + P)
-                group = mx_banks.tile([P, TOKENS], F32, tag="group", name="group")
-                for c in range(PASSES):
+                for c in passes:
                     nc.tensor.matmul_mx(
-                        out=group[:],
+                        out=groups[(g, h)][b][:],
                         lhsT=w_codes[(g, c)][:, cols].bitcast(FP8X4),
                         lhsT_scale=w_scales[(g, c)][:, cols],
                         rhs=x_codes[:, c, :].bitcast(FP8X4),
@@ -214,7 +210,6 @@ def tile_customlstmcell_kernel(
                         start=(c == 0),
                         stop=(c == PASSES - 1),
                     )
-                groups[(g, h)].append(group)
 
         def leave_psum(g, h):
             gate_t[(g, h)] = []
@@ -253,11 +248,11 @@ def tile_customlstmcell_kernel(
                 diff[(h, i)] = bank
 
         def rest_of_h(h):
+            rest = raw_pool.tile([P, TILES, HALF], F32, tag="raw", name="rest")
             for i in range(TILES):
-                bank = token_banks.tile([P, HALF], F32, tag="bank", name="bank")
-                nc.tensor.matmul(out=bank[:], lhsT=ident_bf[:], rhs=hi_sb[:, i, half_cols(h)], start=True, stop=False)
-                nc.tensor.matmul(out=bank[:], lhsT=neg_m_diag[:, i, :], rhs=hi_sb[:, i, half_cols(h)], start=False, stop=True)
-                rest_h[(h, i)] = bank
+                nc.scalar.activation(
+                    out=rest[:, i, :], in_=hi_sb[:, i, half_cols(h)], func=ACT.Identity, scale=one_minus_m[:, i : i + 1])
+                rest_h[(h, i)] = rest[:, i, :]
 
         def gates_if(h, pair):
             for i in pair:
@@ -331,7 +326,7 @@ def tile_customlstmcell_kernel(
                     out=slot(plane_b, h, i),
                     in0=quotient[i][:],
                     scalar=half_m[:, i : i + 1],
-                    in1=rest_h[(h, i)][:],
+                    in1=rest_h[(h, i)],
                     op0=ALU.mult,
                     op1=ALU.add,
                 )
@@ -339,7 +334,7 @@ def tile_customlstmcell_kernel(
 
         slabs = [(g, c) for g in (F, I, Z, O) for c in range(PASSES)]
         loads = slabs[:7] + [("mi", 0), slabs[7], ("ni", 0), ("ci", 0)] + slabs[8:]
-        whole_on_vector = (O, 1)
+        whole_on_vector = (7, 8)
         step = [0]
 
         def next_load():
@@ -355,7 +350,7 @@ def tile_customlstmcell_kernel(
             if n < len(slabs):
                 g, c = slabs[n]
                 grouped[(g, c)] = grouped_pool.tile([P, DFF, PACK], BF16, tag="grouped", name="grouped", align_bytes=64)
-                regroup(g, c, 1, "vector" if (g, c) == whole_on_vector else "scalar")
+                regroup(g, c, 1, "vector" if n in whole_on_vector else "scalar")
 
         def next_slab():
             n = step[0]
@@ -377,18 +372,21 @@ def tile_customlstmcell_kernel(
         next_slab()
         next_slab()
         prepare_biases()
+        products(F, 0, range(0, 1))
         next_slab()
+        products(F, 0, range(1, 2))
         next_slab()
-        products(F, 0)
+        products(F, 0, range(2, 3))
         next_slab()
         leave_psum(F, 0)
+        products(I, 0, range(0, 1))
         next_slab()
+        products(I, 0, range(1, 2))
         next_slab()
-        products(I, 0)
+        products(I, 0, range(2, 3))
         leave_psum(I, 0)
         keep_finite(state[("mi", 0)][:].rearrange("p a b -> p (a b)"))
         prepare_blends()
-        keep_finite(hi_sb[:].rearrange("p a b -> p (a b)"))
 
         for h in range(2):
             ahead = ((F, 1), (I, 1)) if h == 0 else ((Z, 0), (Z, 1))
@@ -430,13 +428,14 @@ def tile_customlstmcell_kernel(
         cell_c(1, PAIRS[1])
         back(O, 0, range(TILES))
         inverse_square(0)
+        rest_of_h(0)
         leave_psum(O, 1)
         inverse_square(1)
+        rest_of_h(1)
 
         for h in range(2):
-            if h == 1:
-                back(O, 1, range(TILES))
             cell_o(h)
-            rest_of_h(h)
+            if h == 0:
+                back(O, 1, range(TILES))
             cell_h(h, PAIRS[0])
             cell_h(h, PAIRS[1])

@@ -71,9 +71,11 @@ def tile_customlstmcell_kernel(
         x_scales = keep.tile([P, PASSES, TOKENS], U8, name="x_scales", align_bytes=64)
         ident = consts.tile([P, P], F32, name="ident")
         neg_ident_bf = consts.tile([P, P], BF16, name="neg_ident_bf")
-        vec_rows = consts.tile([P, P], BF16, name="vec_rows")
-        vec_rows_f = consts.tile([P, P], F32, name="vec_rows_f")
-        vec_cols = consts.tile([P, P], F32, name="vec_cols")
+        vec_rows, vec_rows_f, vec_cols = [], [], []
+        for group in range(2):
+            vec_rows.append(consts.tile([P, P], BF16, name="vec_rows%d" % group))
+            vec_rows_f.append(consts.tile([P, P], F32, name="vec_rows_f%d" % group))
+            vec_cols.append(consts.tile([P, P], F32, name="vec_cols%d" % group))
         bias = consts.tile([P, W_COLS], F32, name="bias")
         neg_bias_f = consts.tile([P, GATE_BLOCKS], F32, name="neg_bias_f")
         half_bias_o = consts.tile([P, GATE_BLOCKS], F32, name="half_bias_o")
@@ -95,7 +97,7 @@ def tile_customlstmcell_kernel(
             return plane[:, TILES * h : TILES * h + TILES, :].rearrange("p a b -> p (a b)")
 
         def m_of(i):
-            return vec_cols[:, M_COL + i : M_COL + i + 1]
+            return vec_cols[0][:, M_COL + i : M_COL + i + 1]
 
         def gate_bias(g):
             return slice(GATE_BLOCKS * g, GATE_BLOCKS * g + GATE_BLOCKS)
@@ -111,13 +113,19 @@ def tile_customlstmcell_kernel(
 
         def load_small():
             make_identity(nc, ident[:])
-            nc.vector.memset(vec_rows[:], 0.0)
-            for v, vec in enumerate(biases):
-                nc.scalar.dma_start(out=vec_rows[gate_bias(v), :], in_=vec.rearrange("(r c) -> r c", c=P))
-            nc.scalar.dma_start(out=vec_rows[M_COL : M_COL + TILES, :], in_=m.rearrange("(r x) p o -> r (x p o)", x=2))
+            nc.vector.memset(vec_rows[0][:], 0.0)
+            nc.vector.memset(vec_rows[1][:], 0.0)
+            load_biases(0, (I, F), nc.scalar)
+            nc.scalar.dma_start(out=vec_rows[0][M_COL : M_COL + TILES, :], in_=m.rearrange("(r x) p o -> r (x p o)", x=2))
+
+        def load_biases(group, gates, engine):
+            for g in gates:
+                for v in (g, 4 + g):
+                    engine.dma_start(out=vec_rows[group][gate_bias(v), :], in_=biases[v].rearrange("(r c) -> r c", c=P))
 
         def load_activations():
-            nc.sync.dma_start(out=hi_sb[:], in_=tiled(Hi))
+            for pair in PAIRS:
+                nc.sync.dma_start(out=hi_sb[:, pair[0] : pair[0] + 2, :], in_=tiled(Hi)[:, pair[0] : pair[0] + 2, :])
             raw["zi"] = raw_pool.tile([P, TILES, K_PASS], BF16, tag="raw", name="zi_sb")
             nc.sync.dma_start(out=raw["zi"][:], in_=tiled(Zi))
 
@@ -127,22 +135,23 @@ def tile_customlstmcell_kernel(
             x_grouped = {}
             for c in range(PASSES):
                 x_grouped[c] = grouped_pool.tile([P, 2, 2 * P * PACK], BF16, tag="grouped", name="x_grouped", align_bytes=64)
-                for two in range(2):
-                    bank = token_banks.tile([P, BANK], F32, tag="bank", name="x_bank")
-                    for u in range(2):
-                        for which in range(2):
-                            i = 2 * two + which
-                            words = hi_words[:, 2 * i + c, :, u] if c < 2 else zi_words[:, i, :, u]
-                            nc.tensor.transpose(bank[:, (2 * u + which) * P : (2 * u + which) * P + P], words, ident[:])
-                    dst = x_grouped[c][:, two, :].bitcast(F32).rearrange("p (r u) -> p r u", u=2)
-                    src = bank[:].rearrange("p (u r) -> p r u", u=2)
-                    if two == 0:
-                        nc.vector.tensor_copy(out=dst, in_=src)
-                    else:
-                        nc.scalar.copy(out=dst, in_=src)
-                if c > 0:
-                    quantise_pass(x_grouped, c - 1)
-            quantise_pass(x_grouped, PASSES - 1)
+            for c, two in ((0, 0), (1, 0), (0, 1), (1, 1), (2, 0), (2, 1)):
+                bank = token_banks.tile([P, BANK], F32, tag="bank", name="x_bank")
+                for u in range(2):
+                    for which in range(2):
+                        i = 2 * two + which
+                        words = hi_words[:, 2 * i + c, :, u] if c < 2 else zi_words[:, i, :, u]
+                        nc.tensor.transpose(bank[:, (2 * u + which) * P : (2 * u + which) * P + P], words, ident[:])
+                dst = x_grouped[c][:, two, :].bitcast(F32).rearrange("p (r u) -> p r u", u=2)
+                src = bank[:].rearrange("p (u r) -> p r u", u=2)
+                if two == 0:
+                    nc.vector.tensor_copy(out=dst, in_=src)
+                else:
+                    nc.scalar.copy(out=dst, in_=src)
+                if (c, two) == (1, 1):
+                    quantise_pass(x_grouped, 0)
+            quantise_pass(x_grouped, 1)
+            quantise_pass(x_grouped, 2)
 
         def quantise_pass(x_grouped, c):
             nc.vector.quantize_mx(
@@ -151,17 +160,24 @@ def tile_customlstmcell_kernel(
                 in_=x_grouped[c][:].rearrange("p a b -> p (a b)"),
             )
 
-        def prepare_biases():
-            nc.vector.tensor_copy(out=vec_rows_f[:], in_=vec_rows[:])
+        def bias_columns(group, gates):
+            nc.vector.tensor_copy(out=vec_rows_f[group][:], in_=vec_rows[group][:])
             bank = token_banks.tile([P, BANK], F32, tag="bank", name="vec_bank")
-            nc.tensor.transpose(bank[:, 0:P], vec_rows_f[:], ident[:])
-            nc.vector.tensor_copy(out=vec_cols[:], in_=bank[:, 0:P])
-            nc.vector.tensor_tensor(out=bias[:], in0=vec_cols[:, 0:W_COLS], in1=vec_cols[:, W_COLS:M_COL], op=ALU.add)
+            nc.tensor.transpose(bank[:, 0:P], vec_rows_f[group][:], ident[:])
+            nc.vector.tensor_copy(out=vec_cols[group][:], in_=bank[:, 0:P])
+            w_cols = slice(GATE_BLOCKS * gates[0], GATE_BLOCKS * gates[-1] + GATE_BLOCKS)
+            r_cols = slice(W_COLS + w_cols.start, W_COLS + w_cols.stop)
+            nc.vector.tensor_tensor(
+                out=bias[:, w_cols], in0=vec_cols[group][:, w_cols], in1=vec_cols[group][:, r_cols], op=ALU.add)
+
+        def prepare_biases():
+            bias_columns(0, (I, F))
             nc.vector.tensor_scalar(out=neg_ident_bf[:], in0=ident[:], scalar1=-1.0, scalar2=None, op0=ALU.mult)
             nc.vector.tensor_scalar(out=neg_bias_f[:], in0=bias[:, gate_bias(F)], scalar1=-1.0, scalar2=None, op0=ALU.mult)
 
         def prepare_blends():
-            m_all = vec_cols[:, M_COL : M_COL + TILES]
+            bias_columns(1, (O, Z))
+            m_all = vec_cols[0][:, M_COL : M_COL + TILES]
             nc.vector.tensor_scalar(out=one_minus_m[:], in0=m_all, scalar1=-1.0, scalar2=1.0, op0=ALU.mult, op1=ALU.add)
             nc.vector.tensor_scalar(out=half_m[:], in0=m_all, scalar1=0.5, scalar2=None, op0=ALU.mult)
             nc.vector.tensor_scalar(out=half_bias_o[:], in0=bias[:, gate_bias(O)], scalar1=0.5, scalar2=None, op0=ALU.mult)
@@ -299,17 +315,19 @@ def tile_customlstmcell_kernel(
         def inverse_square(h):
             nc.scalar.activation(out=half_plane(plane_d, h), in_=half_plane(plane_d, h), func=ACT.Exp, scale=-2.0)
 
+        def cell_z(h):
+            for i in range(TILES):
+                nc.vector.tensor_tensor(out=slot(plane_a, h, i), in0=slot(plane_a, h, i), in1=by_token[(Z, h, i)][:], op=ALU.mult)
+
         def cell_c(h, pair):
-            i_z = {}
-            for i in pair:
-                i_z[i] = pair_pool.tile([P, HALF], F32, tag="first", name="i_z")
-                nc.vector.tensor_tensor(out=i_z[i][:], in0=slot(plane_a, h, i), in1=by_token[(Z, h, i)][:], op=ALU.mult)
             for i in pair:
                 nc.vector.scalar_tensor_tensor(
-                    out=slot(plane_a, h, i), in0=i_z[i][:], scalar=m_of(i), in1=slot(plane_b, h, i), op0=ALU.mult, op1=ALU.add)
+                    out=slot(plane_a, h, i), in0=slot(plane_a, h, i), scalar=m_of(i), in1=slot(plane_b, h, i), op0=ALU.mult, op1=ALU.add)
                 nc.sync.dma_start(out=c_out[tile_rows(i), half_cols(h)], in_=slot(plane_a, h, i))
+
+        def cell_cn(h, pair, engine):
             for i in pair:
-                nc.vector.tensor_tensor(out=slot(plane_b, h, i), in0=slot(plane_a, h, i), in1=slot(plane_c, h, i), op=ALU.mult)
+                engine.tensor_tensor(out=slot(plane_b, h, i), in0=slot(plane_a, h, i), in1=slot(plane_c, h, i), op=ALU.mult)
 
         def cell_o(h):
             for i in range(TILES):
@@ -377,6 +395,7 @@ def tile_customlstmcell_kernel(
         products(F, 0, range(1, 2))
         next_slab()
         products(F, 0, range(2, 3))
+        load_biases(1, (O, Z), nc.sync)
         next_slab()
         leave_psum(F, 0)
         products(I, 0, range(0, 1))
@@ -417,15 +436,21 @@ def tile_customlstmcell_kernel(
 
         back(Z, 0, range(TILES))
         products(O, 0)
-        cell_c(0, PAIRS[0])
+        cell_z(0)
         leave_psum(O, 0)
-        cell_c(0, PAIRS[1])
+        cell_c(0, PAIRS[0])
+        cell_cn(0, PAIRS[0], nc.gpsimd)
         back(Z, 1, range(TILES))
         products(O, 1)
         ln_n(0)
         ln_n(1)
-        cell_c(1, PAIRS[0])
+        cell_z(1)
+        cell_c(0, PAIRS[1])
+        cell_cn(0, PAIRS[1], nc.vector)
         cell_c(1, PAIRS[1])
+        cell_cn(1, PAIRS[1], nc.vector)
+        cell_c(1, PAIRS[0])
+        cell_cn(1, PAIRS[0], nc.gpsimd)
         back(O, 0, range(TILES))
         inverse_square(0)
         rest_of_h(0)

@@ -27,6 +27,7 @@ FLOPS = 2 * TOKENS * (PASSES * K_PASS) * (4 * DFF)
 
 I, F, O, Z = 0, 1, 2, 3
 W_COLS = 4 * GATE_BLOCKS
+WARM_UP = 18
 M_COL = 2 * W_COLS
 FINITE = 3.3895313892515355e38
 
@@ -115,6 +116,7 @@ def tile_customlstmcell_kernel(
             make_identity(nc, ident[:])
             nc.vector.memset(vec_rows[0][:], 0.0)
             nc.vector.memset(vec_rows[1][:], 0.0)
+            nc.vector.tensor_scalar(out=neg_ident_bf[:], in0=ident[:], scalar1=-1.0, scalar2=None, op0=ALU.mult)
             load_biases(0, (I, F), nc.scalar)
             nc.scalar.dma_start(out=vec_rows[0][M_COL : M_COL + TILES, :], in_=m.rearrange("(r x) p o -> r (x p o)", x=2))
 
@@ -128,6 +130,11 @@ def tile_customlstmcell_kernel(
                 nc.sync.dma_start(out=hi_sb[:, pair[0] : pair[0] + 2, :], in_=tiled(Hi)[:, pair[0] : pair[0] + 2, :])
             raw["zi"] = raw_pool.tile([P, TILES, K_PASS], BF16, tag="raw", name="zi_sb")
             nc.sync.dma_start(out=raw["zi"][:], in_=tiled(Zi))
+
+        def warm_up():
+            bank = token_banks.tile([P, BANK], F32, tag="bank", name="warm_bank")
+            for i in range(WARM_UP):
+                nc.tensor.matmul(out=bank[:, 0:P], lhsT=neg_ident_bf[:], rhs=neg_ident_bf[:], start=True, stop=True)
 
         def quantise_activations():
             hi_words = hi_sb[:].rearrange("q i k -> q (i k)").bitcast(F32).rearrange("q (n w u) -> q n w u", w=P, u=2)
@@ -172,14 +179,15 @@ def tile_customlstmcell_kernel(
 
         def prepare_biases():
             bias_columns(0, (I, F))
-            nc.vector.tensor_scalar(out=neg_ident_bf[:], in0=ident[:], scalar1=-1.0, scalar2=None, op0=ALU.mult)
             nc.vector.tensor_scalar(out=neg_bias_f[:], in0=bias[:, gate_bias(F)], scalar1=-1.0, scalar2=None, op0=ALU.mult)
 
         def prepare_blends():
-            bias_columns(1, (O, Z))
             m_all = vec_cols[0][:, M_COL : M_COL + TILES]
             nc.vector.tensor_scalar(out=one_minus_m[:], in0=m_all, scalar1=-1.0, scalar2=1.0, op0=ALU.mult, op1=ALU.add)
             nc.vector.tensor_scalar(out=half_m[:], in0=m_all, scalar1=0.5, scalar2=None, op0=ALU.mult)
+
+        def prepare_late_biases():
+            bias_columns(1, (O, Z))
             nc.vector.tensor_scalar(out=half_bias_o[:], in0=bias[:, gate_bias(O)], scalar1=0.5, scalar2=None, op0=ALU.mult)
 
         def load_slab(g, c):
@@ -187,9 +195,9 @@ def tile_customlstmcell_kernel(
             raw[(g, c)] = raw_pool.tile([P, PACK, DFF], BF16, tag="raw", name="raw")
             nc.sync.dma_start(out=raw[(g, c)][:], in_=src.rearrange("(p j) w -> p j w", j=PACK))
 
-        def regroup(g, c, h, engine):
-            dst = grouped[(g, c)][:, half_cols(h), :].rearrange("p (n r) j -> p n j r", r=8)
-            src = raw[(g, c)][:, :, half_cols(h)].rearrange("p j (n r) -> p n j r", r=8)
+        def regroup(g, c, cols, engine):
+            dst = grouped[(g, c)][:, cols, :].rearrange("p (n r) j -> p n j r", r=8)
+            src = raw[(g, c)][:, :, cols].rearrange("p j (n r) -> p n j r", r=8)
             if engine == "scalar":
                 nc.scalar.copy(out=dst, in_=src)
             else:
@@ -368,14 +376,15 @@ def tile_customlstmcell_kernel(
             if n < len(slabs):
                 g, c = slabs[n]
                 grouped[(g, c)] = grouped_pool.tile([P, DFF, PACK], BF16, tag="grouped", name="grouped", align_bytes=64)
-                regroup(g, c, 1, "vector" if n in whole_on_vector else "scalar")
+                if n not in whole_on_vector:
+                    regroup(g, c, slice(HALF, DFF), "scalar")
 
         def next_slab():
             n = step[0]
             step[0] = n + 1
             second_half(n + 1)
             if n < len(slabs):
-                regroup(slabs[n][0], slabs[n][1], 0, "vector")
+                regroup(slabs[n][0], slabs[n][1], slice(0, DFF if n in whole_on_vector else HALF), "vector")
                 next_load()
             if n > 0:
                 quantise(slabs[n - 1][0], slabs[n - 1][1])
@@ -384,6 +393,7 @@ def tile_customlstmcell_kernel(
         load_activations()
         for fill in range(3):
             next_load()
+        warm_up()
         quantise_activations()
         next_load()
         second_half(0)
@@ -402,6 +412,7 @@ def tile_customlstmcell_kernel(
         next_slab()
         products(I, 0, range(1, 2))
         next_slab()
+        prepare_late_biases()
         products(I, 0, range(2, 3))
         leave_psum(I, 0)
         keep_finite(state[("mi", 0)][:].rearrange("p a b -> p (a b)"))
@@ -438,15 +449,15 @@ def tile_customlstmcell_kernel(
         products(O, 0)
         cell_z(0)
         leave_psum(O, 0)
-        cell_c(0, PAIRS[0])
-        cell_cn(0, PAIRS[0], nc.gpsimd)
+        cell_c(0, PAIRS[1])
+        cell_cn(0, PAIRS[1], nc.vector)
         back(Z, 1, range(TILES))
         products(O, 1)
         ln_n(0)
         ln_n(1)
+        cell_c(0, PAIRS[0])
+        cell_cn(0, PAIRS[0], nc.gpsimd)
         cell_z(1)
-        cell_c(0, PAIRS[1])
-        cell_cn(0, PAIRS[1], nc.vector)
         cell_c(1, PAIRS[1])
         cell_cn(1, PAIRS[1], nc.vector)
         cell_c(1, PAIRS[0])

from contextlib import ExitStack

from concourse import mybir
from concourse.masks import make_identity

F32 = mybir.dt.float32
BF16 = mybir.dt.bfloat16
U32 = mybir.dt.uint32
U8 = mybir.dt.uint8
FP8X4 = mybir.dt.float8_e4m3fn_x4
ALU = mybir.AluOpType
ACT = mybir.ActivationFunctionType

P = 128
PACK = 4
K_PASS = P * PACK
BANK = 512
TOKENS = 512
TILES = TOKENS // P
DFF = 1024
HALF = DFF // 2
BLOCKS = HALF // P
GATE_BLOCKS = DFF // P
PASSES = 3
PAIRS = ((0, 1), (2, 3))
FLOPS = 2 * TOKENS * (PASSES * K_PASS) * (4 * DFF)

I, F, O, Z = 0, 1, 2, 3
W_COLS = 4 * GATE_BLOCKS
WARM_UP = 18
M_COL = 2 * W_COLS
FINITE = 3.3895313892515355e38


def tile_customlstmcell_kernel(
    tc,
    Zi, Ci, Mi, Hi, Ni, m,
    WI_w, WI_b, WF_w, WF_b, WO_w, WO_b, WZ_w, WZ_b,
    RI_w, RI_b, RF_w, RF_b, RO_w, RO_b, RZ_w, RZ_b,
    out_0, out_1, out_2, out_3,
):
    nc = tc.nc
    w_of = {I: WI_w, F: WF_w, O: WO_w, Z: WZ_w}
    r_of = {I: RI_w, F: RF_w, O: RO_w, Z: RZ_w}
    biases = [WI_b, WF_b, WO_b, WZ_b, RI_b, RF_b, RO_b, RZ_b]
    state_of = {"mi": Mi, "ni": Ni, "ci": Ci}

    def rows(ap):
        return ap.rearrange("b p k -> (b p) k")

    def tiled(ap):
        return rows(ap).rearrange("(i q) k -> q i k", q=P)

    c_out, m_out, h_out, n_out = rows(out_0), rows(out_1), rows(out_2), rows(out_3)

    with ExitStack() as ctx:
        consts = ctx.enter_context(tc.tile_pool(name="consts", bufs=1))
        keep = ctx.enter_context(tc.tile_pool(name="keep", bufs=1))
        codes = ctx.enter_context(tc.tile_pool(name="codes", bufs=1))
        gate_pool = ctx.enter_context(tc.tile_pool(name="gate_pool", bufs=2 * BLOCKS))
        raw_pool = ctx.enter_context(tc.tile_pool(name="raw_pool", bufs=4))
        state_pool = ctx.enter_context(tc.tile_pool(name="state_pool", bufs=1))
        grouped_pool = ctx.enter_context(tc.tile_pool(name="grouped_pool", bufs=3))
        planes = ctx.enter_context(tc.tile_pool(name="planes", bufs=1))
        pair_pool = ctx.enter_context(tc.tile_pool(name="pair_pool", bufs=2))
        mx_banks = ctx.enter_context(tc.psum_pool(name="mx_banks", bufs=BLOCKS))
        token_banks = ctx.enter_context(tc.psum_pool(name="token_banks", bufs=TILES))
        ctx.enter_context(tc.manual_schedule())

        hi_sb = keep.tile([P, TILES, DFF], BF16, name="hi_sb")
        x_codes = keep.tile([P, PASSES, TOKENS], U32, name="x_codes", align_bytes=64)
        x_scales = keep.tile([P, PASSES, TOKENS], U8, name="x_scales", align_bytes=64)
        ident = consts.tile([P, P], F32, name="ident")
        neg_ident_bf = consts.tile([P, P], BF16, name="neg_ident_bf")
        vec_rows, vec_rows_f, vec_cols = [], [], []
        for group in range(2):
            vec_rows.append(consts.tile([P, P], BF16, name="vec_rows%d" % group))
            vec_rows_f.append(consts.tile([P, P], F32, name="vec_rows_f%d" % group))
            vec_cols.append(consts.tile([P, P], F32, name="vec_cols%d" % group))
        bias = consts.tile([P, W_COLS], F32, name="bias")
        neg_bias_f = consts.tile([P, GATE_BLOCKS], F32, name="neg_bias_f")
        half_bias_o = consts.tile([P, GATE_BLOCKS], F32, name="half_bias_o")
        one_minus_m = consts.tile([P, TILES], F32, name="one_minus_m")
        half_m = consts.tile([P, TILES], F32, name="half_m")

        plane_a = planes.tile([P, 2 * TILES, HALF], F32, name="plane_a")
        plane_b = planes.tile([P, 2 * TILES, HALF], F32, name="plane_b")
        plane_c = planes.tile([P, 2 * TILES, HALF], F32, name="plane_c")
        plane_d = planes.tile([P, 2 * TILES, HALF], F32, name="plane_d")

        raw, grouped, w_codes, w_scales, state = {}, {}, {}, {}, {}
        groups, gate_t, by_token, diff, rest_h = {}, {}, {}, {}, {}

        def slot(plane, h, i):
            return plane[:, TILES * h + i, :]

        def half_plane(plane, h):
            return plane[:, TILES * h : TILES * h + TILES, :].rearrange("p a b -> p (a b)")

        def m_of(i):
            return vec_cols[0][:, M_COL + i : M_COL + i + 1]

        def gate_bias(g):
            return slice(GATE_BLOCKS * g, GATE_BLOCKS * g + GATE_BLOCKS)

        def half_cols(h):
            return slice(h * HALF, h * HALF + HALF)

        def tile_rows(i):
            return slice(i * P, i * P + P)

        def keep_finite(ap):
            nc.vector.tensor_scalar(out=ap, in0=ap, scalar1=FINITE, scalar2=-FINITE, op0=ALU.min, op1=ALU.max)

        def load_small():
            make_identity(nc, ident[:])
            nc.vector.memset(vec_rows[0][:], 0.0)
            nc.vector.memset(vec_rows[1][:], 0.0)
            nc.vector.tensor_scalar(out=neg_ident_bf[:], in0=ident[:], scalar1=-1.0, scalar2=None, op0=ALU.mult)
            load_biases(0, (I, F), nc.scalar)
            nc.scalar.dma_start(out=vec_rows[0][M_COL : M_COL + TILES, :], in_=m.rearrange("(r x) p o -> r (x p o)", x=2))

        def load_biases(group, gates, engine):
            for g in gates:
                for v in (g, 4 + g):
                    engine.dma_start(out=vec_rows[group][gate_bias(v), :], in_=biases[v].rearrange("(r c) -> r c", c=P))

        def load_activations():
            for pair in PAIRS:
                nc.sync.dma_start(out=hi_sb[:, pair[0] : pair[0] + 2, :], in_=tiled(Hi)[:, pair[0] : pair[0] + 2, :])
            raw["zi"] = raw_pool.tile([P, TILES, K_PASS], BF16, tag="raw", name="zi_sb")
            nc.sync.dma_start(out=raw["zi"][:], in_=tiled(Zi))

        def warm_up():
            bank = token_banks.tile([P, BANK], F32, tag="bank", name="warm_bank")
            for i in range(WARM_UP):
                nc.tensor.matmul(out=bank[:, 0:P], lhsT=neg_ident_bf[:], rhs=neg_ident_bf[:], start=True, stop=True)

        def quantise_activations():
            hi_words = hi_sb[:].rearrange("q i k -> q (i k)").bitcast(F32).rearrange("q (n w u) -> q n w u", w=P, u=2)
            zi_words = raw["zi"][:].rearrange("q i k -> q (i k)").bitcast(F32).rearrange("q (n w u) -> q n w u", w=P, u=2)
            x_grouped = {}
            for c in range(PASSES):
                x_grouped[c] = grouped_pool.tile([P, 2, 2 * P * PACK], BF16, tag="grouped", name="x_grouped", align_bytes=64)
            for c, two in ((0, 0), (1, 0), (0, 1), (1, 1), (2, 0), (2, 1)):
                bank = token_banks.tile([P, BANK], F32, tag="bank", name="x_bank")
                for u in range(2):
                    for which in range(2):
                        i = 2 * two + which
                        words = hi_words[:, 2 * i + c, :, u] if c < 2 else zi_words[:, i, :, u]
                        nc.tensor.transpose(bank[:, (2 * u + which) * P : (2 * u + which) * P + P], words, ident[:])
                dst = x_grouped[c][:, two, :].bitcast(F32).rearrange("p (r u) -> p r u", u=2)
                src = bank[:].rearrange("p (u r) -> p r u", u=2)
                if two == 0:
                    nc.vector.tensor_copy(out=dst, in_=src)
                else:
                    nc.scalar.copy(out=dst, in_=src)
                if (c, two) == (1, 1):
                    quantise_pass(x_grouped, 0)
            quantise_pass(x_grouped, 1)
            quantise_pass(x_grouped, 2)

        def quantise_pass(x_grouped, c):
            nc.vector.quantize_mx(
                out=x_codes[:, c, :].bitcast(FP8X4),
                scales=x_scales[:, c, :],
                in_=x_grouped[c][:].rearrange("p a b -> p (a b)"),
            )

        def bias_columns(group, gates):
            nc.vector.tensor_copy(out=vec_rows_f[group][:], in_=vec_rows[group][:])
            bank = token_banks.tile([P, BANK], F32, tag="bank", name="vec_bank")
            nc.tensor.transpose(bank[:, 0:P], vec_rows_f[group][:], ident[:])
            nc.vector.tensor_copy(out=vec_cols[group][:], in_=bank[:, 0:P])
            w_cols = slice(GATE_BLOCKS * gates[0], GATE_BLOCKS * gates[-1] + GATE_BLOCKS)
            r_cols = slice(W_COLS + w_cols.start, W_COLS + w_cols.stop)
            nc.vector.tensor_tensor(
                out=bias[:, w_cols], in0=vec_cols[group][:, w_cols], in1=vec_cols[group][:, r_cols], op=ALU.add)

        def prepare_biases():
            bias_columns(0, (I, F))
            nc.vector.tensor_scalar(out=neg_bias_f[:], in0=bias[:, gate_bias(F)], scalar1=-1.0, scalar2=None, op0=ALU.mult)

        def prepare_blends():
            m_all = vec_cols[0][:, M_COL : M_COL + TILES]
            nc.vector.tensor_scalar(out=one_minus_m[:], in0=m_all, scalar1=-1.0, scalar2=1.0, op0=ALU.mult, op1=ALU.add)
            nc.vector.tensor_scalar(out=half_m[:], in0=m_all, scalar1=0.5, scalar2=None, op0=ALU.mult)

        def prepare_late_biases():
            bias_columns(1, (O, Z))
            nc.vector.tensor_scalar(out=half_bias_o[:], in0=bias[:, gate_bias(O)], scalar1=0.5, scalar2=None, op0=ALU.mult)

        def load_slab(g, c):
            src = w_of[g][K_PASS * c : K_PASS * c + K_PASS, :] if c < 2 else r_of[g]
            raw[(g, c)] = raw_pool.tile([P, PACK, DFF], BF16, tag="raw", name="raw")
            nc.sync.dma_start(out=raw[(g, c)][:], in_=src.rearrange("(p j) w -> p j w", j=PACK))

        def regroup(g, c, cols, engine):
            dst = grouped[(g, c)][:, cols, :].rearrange("p (n r) j -> p n j r", r=8)
            src = raw[(g, c)][:, :, cols].rearrange("p j (n r) -> p n j r", r=8)
            if engine == "scalar":
                nc.scalar.copy(out=dst, in_=src)
            else:
                nc.vector.tensor_copy(out=dst, in_=src)

        def quantise(g, c):
            w_codes[(g, c)] = codes.tile([P, DFF], U32, name="w_codes%d_%d" % (g, c), align_bytes=64)
            w_scales[(g, c)] = codes.tile([P, DFF], U8, name="w_scales%d_%d" % (g, c), align_bytes=64)
            nc.vector.quantize_mx(
                out=w_codes[(g, c)][:].bitcast(FP8X4),
                scales=w_scales[(g, c)][:],
                in_=grouped[(g, c)][:].rearrange("p w j -> p (w j)"),
            )

        def load_state(name, h):
            state[(name, h)] = state_pool.tile([P, TILES, HALF], BF16, tag=name, name=name)
            nc.sync.dma_start(out=state[(name, h)][:], in_=tiled(state_of[name])[:, :, half_cols(h)])

        def products(g, h, passes=range(PASSES)):
            if (g, h) not in groups:
                groups[(g, h)] = []
                for b in range(BLOCKS):
                    group = mx_banks.tile([P, TOKENS], F32, tag="group", name="group")
                    groups[(g, h)].append(group)
            for b in range(BLOCKS):
                cols = slice((BLOCKS * h + b) * P, (BLOCKS * h + b) * P + P)
                for c in passes:
                    nc.tensor.matmul_mx(
                        out=groups[(g, h)][b][:],
                        lhsT=w_codes[(g, c)][:, cols].bitcast(FP8X4),
                        lhsT_scale=w_scales[(g, c)][:, cols],
                        rhs=x_codes[:, c, :].bitcast(FP8X4),
                        rhs_scale=x_scales[:, c, :],
                        start=(c == 0),
                        stop=(c == PASSES - 1),
                    )

        def leave_psum(g, h):
            gate_t[(g, h)] = []
            for b in range(BLOCKS):
                col = BLOCKS * h + b
                block = gate_pool.tile([P, TOKENS], F32, tag="gate_t", name="gate_t")
                group = groups[(g, h)][b]
                if g == O:
                    func, scale, shift = ACT.Tanh, 0.5, half_bias_o[:, col : col + 1]
                elif g == F:
                    func, scale, shift = ACT.Identity, -1.0, neg_bias_f[:, col : col + 1]
                else:
                    func, scale = (ACT.Tanh if g == Z else ACT.Identity), 1.0
                    shift = bias[:, GATE_BLOCKS * g + col : GATE_BLOCKS * g + col + 1]
                nc.scalar.activation(out=block[:], in_=group[:], func=func, bias=shift, scale=scale)
                gate_t[(g, h)].append(block)

        def back(g, h, tiles):
            for i in tiles:
                bank = token_banks.tile([P, HALF], F32, tag="bank", name="bank")
                for b in range(BLOCKS):
                    nc.tensor.transpose(bank[:, b * P : b * P + P], gate_t[(g, h)][b][:, tile_rows(i)], ident[:])
                by_token[(g, h, i)] = bank

        def difference(h, tiles):
            for i in tiles:
                bank = token_banks.tile([P, HALF], F32, tag="bank", name="bank")
                for b in range(BLOCKS):
                    cols = slice(b * P, b * P + P)
                    a_t = gate_t[(I, h)][b][:, tile_rows(i)]
                    neg_f_t = gate_t[(F, h)][b][:, tile_rows(i)]
                    nc.tensor.matmul(out=bank[:, cols], lhsT=a_t, rhs=ident[:], is_transpose=True, start=True, stop=False)
                    nc.tensor.matmul(out=bank[:, cols], lhsT=neg_f_t, rhs=ident[:], is_transpose=True, start=False, stop=False)
                    nc.tensor.matmul(
                        out=bank[:, cols], lhsT=neg_ident_bf[:], rhs=state[("mi", h)][:, i, cols], start=False, stop=True)
                diff[(h, i)] = bank

        def rest_of_h(h):
            rest = raw_pool.tile([P, TILES, HALF], F32, tag="raw", name="rest")
            for i in range(TILES):
                nc.scalar.activation(
                    out=rest[:, i, :], in_=hi_sb[:, i, half_cols(h)], func=ACT.Identity, scale=one_minus_m[:, i : i + 1])
                rest_h[(h, i)] = rest[:, i, :]

        def gates_if(h, pair):
            for i in pair:
                nc.scalar.activation(out=slot(plane_b, h, i), in_=diff[(h, i)][:], func=ACT.Relu, scale=-1.0)
                nc.scalar.activation(out=slot(plane_c, h, i), in_=diff[(h, i)][:], func=ACT.Exp, scale=-1.0)
            for i in pair:
                nc.scalar.activation(out=slot(plane_a, h, i), in_=slot(plane_b, h, i), func=ACT.Exp, scale=-1.0)

        def cell_m(h, pair):
            for i in pair:
                nc.vector.tensor_tensor(out=slot(plane_d, h, i), in0=by_token[(I, h, i)][:], in1=slot(plane_b, h, i), op=ALU.add)
                nc.sync.dma_start(out=m_out[tile_rows(i), half_cols(h)], in_=slot(plane_d, h, i))

        def cell_n(h, pair):
            f_ni, m_f = {}, {}
            for i in pair:
                f_ni[i] = pair_pool.tile([P, HALF], F32, tag="first", name="f_ni")
                nc.vector.scalar_tensor_tensor(
                    out=f_ni[i][:], in0=slot(plane_c, h, i), scalar=1.0, in1=state[("ni", h)][:, i, :], op0=ALU.min, op1=ALU.mult)
            for i in pair:
                m_f[i] = pair_pool.tile([P, HALF], F32, tag="second", name="m_f")
                nc.vector.tensor_scalar(
                    out=m_f[i][:], in0=slot(plane_c, h, i), scalar1=1.0, scalar2=m_of(i), op0=ALU.min, op1=ALU.mult)
            for i in pair:
                nc.vector.tensor_tensor(out=slot(plane_c, h, i), in0=slot(plane_a, h, i), in1=f_ni[i][:], op=ALU.add)
                nc.sync.dma_start(out=n_out[tile_rows(i), half_cols(h)], in_=slot(plane_c, h, i))
            for i in pair:
                nc.vector.scalar_tensor_tensor(
                    out=slot(plane_b, h, i),
                    in0=m_f[i][:],
                    scalar=one_minus_m[:, i : i + 1],
                    in1=state[("ci", h)][:, i, :],
                    op0=ALU.add,
                    op1=ALU.mult,
                )

        def abs_n(h, pair):
            for i in pair:
                nc.scalar.activation(out=slot(plane_d, h, i), in_=slot(plane_c, h, i), func=ACT.Abs)

        def ln_n(h):
            nc.scalar.activation(out=half_plane(plane_d, h), in_=half_plane(plane_d, h), func=ACT.Ln)

        def inverse_square(h):
            nc.scalar.activation(out=half_plane(plane_d, h), in_=half_plane(plane_d, h), func=ACT.Exp, scale=-2.0)

        def cell_z(h):
            for i in range(TILES):
                nc.vector.tensor_tensor(out=slot(plane_a, h, i), in0=slot(plane_a, h, i), in1=by_token[(Z, h, i)][:], op=ALU.mult)

        def cell_c(h, pair):
            for i in pair:
                nc.vector.scalar_tensor_tensor(
                    out=slot(plane_a, h, i), in0=slot(plane_a, h, i), scalar=m_of(i), in1=slot(plane_b, h, i), op0=ALU.mult, op1=ALU.add)
                nc.sync.dma_start(out=c_out[tile_rows(i), half_cols(h)], in_=slot(plane_a, h, i))

        def cell_cn(h, pair, engine):
            for i in pair:
                engine.tensor_tensor(out=slot(plane_b, h, i), in0=slot(plane_a, h, i), in1=slot(plane_c, h, i), op=ALU.mult)

        def cell_o(h):
            for i in range(TILES):
                nc.vector.scalar_tensor_tensor(
                    out=slot(plane_b, h, i), in0=by_token[(O, h, i)][:], scalar=1.0, in1=slot(plane_b, h, i), op0=ALU.add, op1=ALU.mult)

        def cell_h(h, pair):
            quotient = {}
            for i in pair:
                quotient[i] = pair_pool.tile([P, HALF], F32, tag="second", name="quotient")
                nc.vector.tensor_tensor(out=quotient[i][:], in0=slot(plane_b, h, i), in1=slot(plane_d, h, i), op=ALU.mult)
            for i in pair:
                nc.vector.scalar_tensor_tensor(
                    out=slot(plane_b, h, i),
                    in0=quotient[i][:],
                    scalar=half_m[:, i : i + 1],
                    in1=rest_h[(h, i)],
                    op0=ALU.mult,
                    op1=ALU.add,
                )
                nc.sync.dma_start(out=h_out[tile_rows(i), half_cols(h)], in_=slot(plane_b, h, i))

        slabs = [(g, c) for g in (F, I, Z, O) for c in range(PASSES)]
        loads = slabs[:7] + [("mi", 0), slabs[7], ("ni", 0), ("ci", 0)] + slabs[8:]
        whole_on_vector = (7, 8)
        step = [0]

        def next_load():
            while loads:
                what, index = loads.pop(0)
                if what in state_of:
                    load_state(what, index)
                else:
                    load_slab(what, index)
                    break

        def second_half(n):
            if n < len(slabs):
                g, c = slabs[n]
                grouped[(g, c)] = grouped_pool.tile([P, DFF, PACK], BF16, tag="grouped", name="grouped", align_bytes=64)
                if n not in whole_on_vector:
                    regroup(g, c, slice(HALF, DFF), "scalar")

        def next_slab():
            n = step[0]
            step[0] = n + 1
            second_half(n + 1)
            if n < len(slabs):
                regroup(slabs[n][0], slabs[n][1], slice(0, DFF if n in whole_on_vector else HALF), "vector")
                next_load()
            if n > 0:
                quantise(slabs[n - 1][0], slabs[n - 1][1])

        load_small()
        load_activations()
        for fill in range(3):
            next_load()
        warm_up()
        quantise_activations()
        next_load()
        second_half(0)
        next_slab()
        next_slab()
        prepare_biases()
        products(F, 0, range(0, 1))
        next_slab()
        products(F, 0, range(1, 2))
        next_slab()
        products(F, 0, range(2, 3))
        load_biases(1, (O, Z), nc.sync)
        next_slab()
        leave_psum(F, 0)
        products(I, 0, range(0, 1))
        next_slab()
        products(I, 0, range(1, 2))
        next_slab()
        prepare_late_biases()
        products(I, 0, range(2, 3))
        leave_psum(I, 0)
        keep_finite(state[("mi", 0)][:].rearrange("p a b -> p (a b)"))
        prepare_blends()

        for h in range(2):
            ahead = ((F, 1), (I, 1)) if h == 0 else ((Z, 0), (Z, 1))
            difference(h, PAIRS[0])
            back(I, h, PAIRS[0])
            gates_if(h, PAIRS[0])
            next_slab()
            cell_m(h, PAIRS[0])
            difference(h, PAIRS[1])
            back(I, h, PAIRS[1])
            gates_if(h, PAIRS[1])
            if h == 0:
                load_state("mi", 1)
            next_slab()
            for which in range(2):
                products(ahead[which][0], ahead[which][1])
                leave_psum(ahead[which][0], ahead[which][1])
                cell_n(h, PAIRS[which])
                abs_n(h, PAIRS[which])
                if which == 0:
                    next_slab()
                    cell_m(h, PAIRS[1])
                    if h == 0:
                        keep_finite(state[("mi", 1)][:].rearrange("p a b -> p (a b)"))
            if h == 0:
                load_state("ni", 1)
                load_state("ci", 1)

        back(Z, 0, range(TILES))
        products(O, 0)
        cell_z(0)
        leave_psum(O, 0)
        cell_c(0, PAIRS[1])
        cell_cn(0, PAIRS[1], nc.vector)
        back(Z, 1, range(TILES))
        products(O, 1)
        ln_n(0)
        ln_n(1)
        cell_c(0, PAIRS[0])
        cell_cn(0, PAIRS[0], nc.gpsimd)
        cell_z(1)
        cell_c(1, PAIRS[1])
        cell_cn(1, PAIRS[1], nc.vector)
        cell_c(1, PAIRS[0])
        cell_cn(1, PAIRS[0], nc.gpsimd)
        back(O, 0, range(TILES))
        inverse_square(0)
        rest_of_h(0)
        leave_psum(O, 1)
        inverse_square(1)
        rest_of_h(1)

        for h in range(2):
            cell_o(h)
            if h == 0:
                back(O, 1, range(TILES))
            cell_h(h, PAIRS[0])
            cell_h(h, PAIRS[1])
